import numpy as np
import ml_dtypes


def mxq(x, axis, fmt="e4m3"):
    dtype, down = {"e4m3": (ml_dtypes.float8_e4m3fn, 7), "e5m2": (ml_dtypes.float8_e5m2, 14)}[fmt]
    v = np.moveaxis(np.asarray(x, np.float32).astype(ml_dtypes.bfloat16).astype(np.float64), axis, -1)
    blocks = v.reshape(v.shape[:-1] + (-1, 32))
    amax = np.abs(blocks).max(-1, keepdims=True)
    byte = np.maximum(np.where(amax > 0, np.frexp(amax)[1] - 1 + 127, 0) - down, 1)
    scale = np.exp2(byte - 127.0)
    codes = (blocks / scale).astype(np.float32).astype(dtype).astype(np.float64)
    return np.moveaxis((codes * scale).reshape(v.shape), -1, axis)


WIDE = False


def mx_kscale(k):
    if not WIDE:
        return np.ones(k)
    levels = np.array([10, -10, 5, -5, 0])
    a = np.random.permutation(np.resize(levels, k // 512 * 4)).reshape(k // 512, 4)
    idx = np.arange(k)
    return np.exp2(a[idx // 512, idx % 128 // 32])


BF16 = ml_dtypes.bfloat16


def bf(x):
    return np.asarray(x, np.float32).astype(BF16)


def f64(x):
    return np.asarray(x).astype(np.float64)


B, S, E, H = 4, 256, 1024, 16
DH = E // H
EPS = 1e-5


def heads(t):
    return t.reshape(B, S, H, DH).transpose(0, 2, 1, 3)


def setup_inputs():
    s = mx_kscale(E)
    tok = np.exp2(np.random.uniform(-7.5, 1.5, (B, S, 1)))
    off = 0.5 * np.random.standard_normal((B, S, 1))
    return {"inputs": bf((np.random.standard_normal((B, S, E)) + off) * tok),
            "ln_w": bf((1.0 + 0.1 * np.random.standard_normal(E)) * s),
            "ln_b": bf(0.1 * np.random.standard_normal(E) * s),
            "w_qkv": bf(np.random.standard_normal((3 * E, E)) / np.sqrt(E) / s[None, :])}


def reference(inputs, ln_w, ln_b, w_qkv):
    a = f64(inputs)
    mu = a.mean(-1, keepdims=True)
    var = a.var(-1, keepdims=True)
    x = (a - mu) / np.sqrt(var + EPS) * f64(ln_w) + f64(ln_b)
    qkv = mxq(x, 2, "e4m3") @ mxq(f64(w_qkv), 1, "e4m3").T
    q, k, v = np.split(qkv, 3, axis=-1)
    return heads(q), heads(k), heads(v)

@@ -1,0 +1,214 @@
+from contextlib import ExitStack
+
+import concourse.bass as bass
+import concourse.mybir as mybir
+import concourse.tile as tile
+from concourse.masks import make_identity
+
+FLOPS = 2 * 1024 * 3072 * 1024
+
+F32 = mybir.dt.float32
+BF16 = mybir.dt.bfloat16
+U32 = mybir.dt.uint32
+U8 = mybir.dt.uint8
+FP8X4 = mybir.dt.float8_e4m3fn_x4
+ALU = mybir.AluOpType
+ACT = mybir.ActivationFunctionType
+
+P = 128
+B = 4
+E = 1024
+EPS = 1e-5
+NJ = 8
+NC = 6
+
+
+def tile_selfattention_pa_kernel(tc, inputs, ln_w, ln_b, w_qkv, out_0, out_1, out_2):
+    nc = tc.nc
+    outs = (out_0, out_1, out_2)
+    with ExitStack() as ctx:
+        const = ctx.enter_context(tc.tile_pool(name="const", bufs=1))
+        wraw_pool = ctx.enter_context(tc.tile_pool(name="wraw", bufs=NC))
+        gw_pool = ctx.enter_context(tc.tile_pool(name="gw", bufs=2))
+        xh_pool = ctx.enter_context(tc.tile_pool(name="xh", bufs=6))
+        pl_pool = ctx.enter_context(tc.tile_pool(name="pl", bufs=2))
+        gx_pool = ctx.enter_context(tc.tile_pool(name="gx", bufs=2))
+        o_pool = ctx.enter_context(tc.tile_pool(name="o", bufs=3))
+        tp_pool = ctx.enter_context(tc.psum_pool(name="tp", bufs=4))
+        acc_pool = ctx.enter_context(tc.psum_pool(name="acc", bufs=4))
+
+        ident = const.tile([P, P], F32)
+        make_identity(nc, ident[:])
+        one = const.tile([P, 1], F32)
+        nc.vector.memset(one[:], 1.0)
+        warm = const.tile([P, 1], F32)
+        nc.scalar.activation(out=warm[:], in_=one[:], func=ACT.Sqrt)
+
+        lnrow = const.tile([P, 256], BF16)
+        nc.vector.memset(lnrow[:], 0.0)
+        nc.scalar.dma_start(out=lnrow[0:4, :], in_=ln_w.rearrange("(r c) -> r c", c=256))
+        nc.scalar.dma_start(out=lnrow[4:8, :], in_=ln_b.rearrange("(r c) -> r c", c=256))
+
+        x_sb = const.tile([P, NJ, E], BF16)
+        for half in range(2):
+            js = slice(4 * half, 4 * half + 4)
+            for b in range(B):
+                nc.sync.dma_start(
+                    out=x_sb[b:P:4, js, :],
+                    in_=inputs[b].rearrange("(pp j) k -> pp j k", j=NJ)[:, js, :],
+                )
+        wraw = []
+        for c in range(NC):
+            w_t = wraw_pool.tile([P, 4 * E], BF16, name="wraw_t", tag="wraw")
+            nc.sync.dma_start(
+                out=w_t[:].rearrange("p (r k) -> p r k", r=4),
+                in_=w_qkv[512 * c : 512 * c + 512, :].rearrange("(r p) k -> p r k", p=P),
+            )
+            wraw.append(w_t)
+
+        lnf = const.tile([P, 2, P], F32)
+        nc.vector.tensor_copy(out=lnf[:], in_=lnrow[:].rearrange("p (q e) -> p e q", e=2))
+        lnt = tp_pool.tile([P, 4, P], F32, name="lnt", tag="tp")
+        for e in range(2):
+            nc.tensor.transpose(lnt[:, e, :], lnf[:, e, :], ident[:])
+        wb = const.tile([P, 2, 8], F32)
+        nc.vector.tensor_copy(out=wb[:], in_=lnt[:, 0:2, 0:8])
+
+        xc = const.tile([P, 2 * 2 * 512], U32, align_bytes=64)
+        xs = const.tile([P, 2 * 2 * 512], U8, align_bytes=64)
+        wc = const.tile([P, NC * 1024], U32, align_bytes=64)
+        ws = const.tile([P, NC * 1024], U8, align_bytes=64)
+
+        st = const.tile([P, NJ, 2, 6], F32)
+        mv = const.tile([P, NJ, 2], F32)
+        std = const.tile([P, NJ], F32)
+        rstd = const.tile([P, NJ], F32)
+        negmu = const.tile([P, NJ], F32)
+        xh = {}
+
+        def stats(j):
+            for h in range(2):
+                nc.vector.bn_stats(out=st[:, j, h, :], in_=x_sb[:, j, 512 * h : 512 * h + 512])
+            nc.vector.bn_aggr(out=mv[:, j, :], in_=st[:, j, :, :].rearrange("p a b -> p (a b)"))
+            nc.scalar.activation(out=std[:, j : j + 1], in_=mv[:, j, 1:2], func=ACT.Sqrt, bias=EPS)
+            nc.vector.reciprocal(out=rstd[:, j : j + 1], in_=std[:, j : j + 1])
+            nc.vector.tensor_scalar_mul(out=negmu[:, j : j + 1], in0=mv[:, j, 0:1], scalar1=-1.0)
+
+        def xhat(j):
+            t = xh_pool.tile([P, 8, P], F32, name="xh_t", tag="xh")
+            nc.gpsimd.tensor_scalar(
+                out=t[:].rearrange("p (gu e) q -> p gu e q", e=2),
+                in0=x_sb[:, j, :].rearrange("p (gu q e) -> p gu e q", gu=4, e=2),
+                scalar1=negmu[:, j : j + 1],
+                scalar2=rstd[:, j : j + 1],
+                op0=ALU.add,
+                op1=ALU.mult,
+            )
+            xh[j] = t
+
+        def xquad(q):
+            for g in range(2):
+                planes = pl_pool.tile([P, 4, 512], BF16, name="planes", tag="pl")
+                for t in range(4):
+                    u, e = t // 2, t % 2
+                    gu = 2 * g + u
+                    xt = tp_pool.tile([P, 4, P], F32, name="xt", tag="tp")
+                    for jq in range(4):
+                        nc.tensor.transpose(xt[:, jq, :], xh[4 * q + jq][:, 2 * gu + e, :], ident[:])
+                    nc.scalar.activation(
+                        out=planes[:, t, :],
+                        in_=xt[:].rearrange("p a b -> p (a b)"),
+                        func=ACT.Identity,
+                        scale=wb[:, e, gu : gu + 1],
+                        bias=wb[:, e, 4 + gu : 5 + gu],
+                    )
+                gx = gx_pool.tile([P, 512, 4], BF16, name="gx", tag="gx", align_bytes=64)
+                nc.vector.tensor_copy(
+                    out=gx[:].rearrange("p (c i) t -> p c t i", i=4),
+                    in_=planes[:].rearrange("p t (c i) -> p c t i", i=4),
+                )
+                sl = slice((2 * q + g) * 512, (2 * q + g) * 512 + 512)
+                nc.vector.quantize_mx(
+                    out=xc[:, sl].bitcast(FP8X4),
+                    scales=xs[:, sl],
+                    in_=gx[:].rearrange("p n t -> p (n t)"),
+                )
+
+        def wprep(c, engines):
+            gw = gw_pool.tile([P, 4096], BF16, name="gw", tag="gw", align_bytes=64)
+            gwf = gw[:].bitcast(F32).rearrange("p (g n u) -> p g n u", g=2, u=2)
+            wf = wraw[c][:].bitcast(F32)
+            for r in range(4):
+                wt = tp_pool.tile([P, 4, P], F32, name="wt", tag="tp")
+                for gu in range(4):
+                    nc.tensor.transpose(wt[:, gu, :], wf[:, 512 * r + P * gu : 512 * r + P * gu + P], ident[:])
+                src = wt[:].rearrange("p (g u) f -> p g f u", u=2)
+                dst = gwf[:, :, P * r : P * r + P, :]
+                if engines[r] == "v":
+                    nc.vector.tensor_copy(out=dst, in_=src)
+                else:
+                    nc.scalar.copy(out=dst, in_=src)
+            sl = slice(c * 1024, c * 1024 + 1024)
+            nc.vector.quantize_mx(out=wc[:, sl].bitcast(FP8X4), scales=ws[:, sl], in_=gw[:])
+
+        o_tiles = {}
+
+        def mx(c, q, engines):
+            if c not in o_tiles:
+                o_tiles[c] = o_pool.tile([P, 8, NJ, 64], F32, name="o_t", tag="o")
+            o_t = o_tiles[c]
+            for jq in range(4):
+                acc = acc_pool.tile([P, 512], F32, name="acc", tag="acc")
+                for g in range(2):
+                    xo = (2 * q + g) * 512 + P * jq
+                    wo = c * 1024 + 512 * g
+                    nc.tensor.matmul_mx(
+                        out=acc[:],
+                        lhsT=xc[:, xo : xo + P].bitcast(FP8X4),
+                        lhsT_scale=xs[:, xo : xo + P],
+                        rhs=wc[:, wo : wo + 512].bitcast(FP8X4),
+                        rhs_scale=ws[:, wo : wo + 512],
+                        start=(g == 0),
+                        stop=(g == 1),
+                    )
+                dst = o_t[:, :, 4 * q + jq, :]
+                src = acc[:].rearrange("p (h d) -> p h d", d=64)
+                if engines[jq] == "v":
+                    nc.vector.tensor_copy(out=dst, in_=src)
+                else:
+                    nc.scalar.copy(out=dst, in_=src)
+
+        def store(c, j0, j1):
+            o_t = o_tiles[c]
+            h0 = 8 * (c % 2)
+            for b in range(B):
+                nc.sync.dma_start(
+                    out=outs[c // 2][b, h0 : h0 + 8, :, :].rearrange("h (pp j) d -> pp h j d", j=NJ)[:, :, j0:j1, :],
+                    in_=o_t[b:P:4, :, j0:j1, :],
+                )
+
+        for j in range(NJ):
+            stats(j)
+            xhat(j)
+        wprep(0, "ssss")
+        xquad(0)
+        wprep(1, "ssss")
+        mx(0, 0, "sssv")
+        mx(1, 0, "sssv")
+        xquad(1)
+        wprep(2, "vvvv")
+        mx(0, 1, "sssv")
+        store(0, 0, 8)
+        mx(1, 1, "sssv")
+        store(1, 0, 8)
+        for c in range(2, NC):
+            if c + 1 < NC:
+                wprep(c + 1, "vvvv")
+            mx(c, 0, "sssv")
+            if c == NC - 1:
+                store(c, 0, 4)
+            mx(c, 1, "sssv")
+            if c == NC - 1:
+                store(c, 4, 8)
+            else:
+                store(c, 0, 8)

@@ -1,8 +1,6 @@
 from contextlib import ExitStack
 
-import concourse.bass as bass
 import concourse.mybir as mybir
-import concourse.tile as tile
 from concourse.masks import make_identity
 
 FLOPS = 2 * 1024 * 3072 * 1024
@@ -22,6 +20,34 @@ EPS = 1e-5
 NJ = 8
 NC = 6
 
+ORDER = (
+    "ldx0b0", "ms", "warm", "ident", "ldln", "ldx0b1", "ldx0b2", "ldx0b3", "lnf", "ldx1b0", "lnT", "wb",
+    "ldx1b1", "ldx1b2", "st0", "ldx1b3", "ldw0", "st1", "sq0", "rs0", "sq1", "st2", "xh0", "ldw1",
+    "rs1", "sq2", "st3", "xh1", "tw00", "tw01", "rs2", "sq3", "st4", "xh2", "ew00s", "tw02",
+    "tw03", "ldw2", "ew01s", "rs3", "ew02s", "st5", "xh3", "sq4", "ew03s", "tw10", "tw11", "rs4",
+    "ew10s", "tw12", "st6", "xh4", "tx000", "ldw3", "sq5", "tx001", "ew11s", "tx002", "rs5", "ex000s",
+    "tx003", "st7", "xh5", "tx010", "sq6", "tx011", "ex001s", "rs6", "ex002v", "sq7", "tx012", "ex003s",
+    "ldw4", "rs7", "tx013", "ex010v", "ex011s", "tw13", "rg00", "ex012s", "ex013s", "qw0", "ldw5", "ew12s",
+    "ew13s", "rg01", "tw20", "tw21", "ew20s", "tw22", "tw23", "qx00", "xh6", "ew21s", "qx01", "ew22s",
+    "qw1", "ew23s", "xh7", "mx00", "mx01", "qw2", "ev00s", "mx02", "ev01s", "tx100", "ev02v", "tx101",
+    "ex100s", "tx102", "ex101v", "tx103", "tx110", "ex102s", "ex103v", "tx111", "tx112", "ex110s", "ex111v", "tx113",
+    "mx03", "ex112s", "rg10", "mx10", "ex113s", "mx11", "ev03v", "ev10s", "mx12", "rg11", "ev11s", "so000",
+    "mx13", "ev12s", "so001", "mx20", "qx10", "ev13s", "mx21", "so002", "ev20s", "qx11", "mx22", "so003",
+    "ev21s", "mx23", "so100", "ev22v", "mx04", "ev23s", "so101", "mx05", "ev04v", "so102", "mx06", "ev05s",
+    "mx07", "so103", "ev06v", "mx14", "so200", "ev07s", "mx15", "so201", "ev14v", "mx16", "ev15s", "so040",
+    "mx17", "ev16v", "so041", "tw30", "ev17s", "tw31", "so042", "ew30v", "tw32", "ew31s", "tw33", "so043",
+    "ew32v", "mx24", "ew33s", "so140", "mx25", "qw3", "ev24s", "mx26", "so141", "ev25s", "mx27", "so142",
+    "ev26s", "tw40", "so143", "ev27v", "tw41", "ew40s", "tw42", "so202", "ew41v", "tw43", "ew42s", "mx30",
+    "so203", "ew43v", "mx31", "so240", "ev30v", "mx32", "ev31s", "qw4", "so241", "mx33", "ev32s", "so242",
+    "mx34", "ev33s", "mx35", "so243", "ev34v", "mx36", "so300", "ev35s", "mx37", "so301", "ev36v", "mx40",
+    "ev37s", "so302", "mx41", "ev40v", "so303", "mx42", "ev41s", "mx43", "so340", "ev42v", "tw50", "so341",
+    "ev43s", "tw51", "ew50v", "tw52", "so342", "ew51s", "tw53", "ew52v", "mx44", "so343", "ew53s", "mx45",
+    "so400", "qw5", "ev44s", "mx46", "so401", "ev45s", "mx47", "ev46s", "so402", "mx50", "ev47v", "so403",
+    "mx51", "ev50v", "so440", "mx52", "ev51s", "so441", "mx53", "ev52v", "mx54", "so442", "ev53s", "mx55",
+    "so443", "ev54v", "mx56", "ev55s", "so500", "mx57", "ev56v", "so501", "ev57s", "so502", "so503", "so540",
+    "so541", "so542", "so543",
+)
+
 
 def tile_selfattention_pa_kernel(tc, inputs, ln_w, ln_b, w_qkv, out_0, out_1, out_2):
     nc = tc.nc
@@ -31,184 +57,181 @@ def tile_selfattention_pa_kernel(tc, inputs, ln_w, ln_b, w_qkv, out_0, out_1, ou
         wraw_pool = ctx.enter_context(tc.tile_pool(name="wraw", bufs=NC))
         gw_pool = ctx.enter_context(tc.tile_pool(name="gw", bufs=2))
         xh_pool = ctx.enter_context(tc.tile_pool(name="xh", bufs=6))
-        pl_pool = ctx.enter_context(tc.tile_pool(name="pl", bufs=2))
-        gx_pool = ctx.enter_context(tc.tile_pool(name="gx", bufs=2))
+        pl_pool = ctx.enter_context(tc.tile_pool(name="pl", bufs=3))
+        gx_pool = ctx.enter_context(tc.tile_pool(name="gx", bufs=3))
         o_pool = ctx.enter_context(tc.tile_pool(name="o", bufs=3))
-        tp_pool = ctx.enter_context(tc.psum_pool(name="tp", bufs=4))
-        acc_pool = ctx.enter_context(tc.psum_pool(name="acc", bufs=4))
+        ps_pool = ctx.enter_context(tc.psum_pool(name="ps", bufs=8))
+        ctx.enter_context(tc.manual_schedule())
 
         ident = const.tile([P, P], F32)
-        make_identity(nc, ident[:])
         one = const.tile([P, 1], F32)
-        nc.vector.memset(one[:], 1.0)
         warm = const.tile([P, 1], F32)
-        nc.scalar.activation(out=warm[:], in_=one[:], func=ACT.Sqrt)
-
         lnrow = const.tile([P, 256], BF16)
-        nc.vector.memset(lnrow[:], 0.0)
-        nc.scalar.dma_start(out=lnrow[0:4, :], in_=ln_w.rearrange("(r c) -> r c", c=256))
-        nc.scalar.dma_start(out=lnrow[4:8, :], in_=ln_b.rearrange("(r c) -> r c", c=256))
-
-        x_sb = const.tile([P, NJ, E], BF16)
-        for half in range(2):
-            js = slice(4 * half, 4 * half + 4)
-            for b in range(B):
-                nc.sync.dma_start(
-                    out=x_sb[b:P:4, js, :],
-                    in_=inputs[b].rearrange("(pp j) k -> pp j k", j=NJ)[:, js, :],
-                )
-        wraw = []
-        for c in range(NC):
-            w_t = wraw_pool.tile([P, 4 * E], BF16, name="wraw_t", tag="wraw")
-            nc.sync.dma_start(
-                out=w_t[:].rearrange("p (r k) -> p r k", r=4),
-                in_=w_qkv[512 * c : 512 * c + 512, :].rearrange("(r p) k -> p r k", p=P),
-            )
-            wraw.append(w_t)
-
         lnf = const.tile([P, 2, P], F32)
-        nc.vector.tensor_copy(out=lnf[:], in_=lnrow[:].rearrange("p (q e) -> p e q", e=2))
-        lnt = tp_pool.tile([P, 4, P], F32, name="lnt", tag="tp")
-        for e in range(2):
-            nc.tensor.transpose(lnt[:, e, :], lnf[:, e, :], ident[:])
         wb = const.tile([P, 2, 8], F32)
-        nc.vector.tensor_copy(out=wb[:], in_=lnt[:, 0:2, 0:8])
-
+        x_sb = const.tile([P, NJ, E], BF16)
         xc = const.tile([P, 2 * 2 * 512], U32, align_bytes=64)
         xs = const.tile([P, 2 * 2 * 512], U8, align_bytes=64)
         wc = const.tile([P, NC * 1024], U32, align_bytes=64)
         ws = const.tile([P, NC * 1024], U8, align_bytes=64)
-
         st = const.tile([P, NJ, 2, 6], F32)
         mv = const.tile([P, NJ, 2], F32)
         std = const.tile([P, NJ], F32)
         rstd = const.tile([P, NJ], F32)
         negmu = const.tile([P, NJ], F32)
-        xh = {}
+        live = {}
 
-        def stats(j):
-            for h in range(2):
-                nc.vector.bn_stats(out=st[:, j, h, :], in_=x_sb[:, j, 512 * h : 512 * h + 512])
-            nc.vector.bn_aggr(out=mv[:, j, :], in_=st[:, j, :, :].rearrange("p a b -> p (a b)"))
-            nc.scalar.activation(out=std[:, j : j + 1], in_=mv[:, j, 1:2], func=ACT.Sqrt, bias=EPS)
-            nc.vector.reciprocal(out=rstd[:, j : j + 1], in_=std[:, j : j + 1])
-            nc.vector.tensor_scalar_mul(out=negmu[:, j : j + 1], in0=mv[:, j, 0:1], scalar1=-1.0)
+        def copy_on(eng, dst, src):
+            if eng == "v":
+                nc.vector.tensor_copy(out=dst, in_=src)
+            else:
+                nc.scalar.copy(out=dst, in_=src)
 
-        def xhat(j):
-            t = xh_pool.tile([P, 8, P], F32, name="xh_t", tag="xh")
-            nc.gpsimd.tensor_scalar(
-                out=t[:].rearrange("p (gu e) q -> p gu e q", e=2),
-                in0=x_sb[:, j, :].rearrange("p (gu q e) -> p gu e q", gu=4, e=2),
-                scalar1=negmu[:, j : j + 1],
-                scalar2=rstd[:, j : j + 1],
-                op0=ALU.add,
-                op1=ALU.mult,
-            )
-            xh[j] = t
+        def bank(key):
+            t = ps_pool.tile([P, 4, P], F32, name="bank", tag="ps")
+            live[key] = t
+            return t
 
-        def xquad(q):
-            for g in range(2):
-                planes = pl_pool.tile([P, 4, 512], BF16, name="planes", tag="pl")
-                for t in range(4):
-                    u, e = t // 2, t % 2
-                    gu = 2 * g + u
-                    xt = tp_pool.tile([P, 4, P], F32, name="xt", tag="tp")
-                    for jq in range(4):
-                        nc.tensor.transpose(xt[:, jq, :], xh[4 * q + jq][:, 2 * gu + e, :], ident[:])
-                    nc.scalar.activation(
-                        out=planes[:, t, :],
-                        in_=xt[:].rearrange("p a b -> p (a b)"),
-                        func=ACT.Identity,
-                        scale=wb[:, e, gu : gu + 1],
-                        bias=wb[:, e, 4 + gu : 5 + gu],
+        for tok in ORDER:
+            kind = tok[0:2]
+            if tok == "ident":
+                make_identity(nc, ident[:])
+            elif tok == "ms":
+                nc.vector.memset(one[:], 1.0)
+                nc.vector.memset(lnrow[:], 0.0)
+            elif tok == "warm":
+                nc.scalar.activation(out=warm[:], in_=one[:], func=ACT.Sqrt)
+            elif tok == "ldln":
+                nc.scalar.dma_start(out=lnrow[0:4, :], in_=ln_w.rearrange("(r c) -> r c", c=256))
+                nc.scalar.dma_start(out=lnrow[4:8, :], in_=ln_b.rearrange("(r c) -> r c", c=256))
+            elif tok == "lnf":
+                nc.vector.tensor_copy(out=lnf[:], in_=lnrow[:].rearrange("p (q e) -> p e q", e=2))
+            elif tok == "lnT":
+                t = bank("ln")
+                for e in range(2):
+                    nc.tensor.transpose(t[:, e, :], lnf[:, e, :], ident[:])
+            elif tok == "wb":
+                nc.vector.tensor_copy(out=wb[:], in_=live["ln"][:, 0:2, 0:8])
+            elif tok[0:3] == "ldx":
+                q, b = int(tok[3]), int(tok[5])
+                js = slice(4 * q, 4 * q + 4)
+                nc.sync.dma_start(
+                    out=x_sb[b:P:4, js, :],
+                    in_=inputs[b].rearrange("(pp j) k -> pp j k", j=NJ)[:, js, :],
+                )
+            elif tok[0:3] == "ldw":
+                c = int(tok[3])
+                w_t = wraw_pool.tile([P, 4 * E], BF16, name="wraw_t", tag="wraw")
+                live["wraw%d" % c] = w_t
+                nc.sync.dma_start(
+                    out=w_t[:].rearrange("p (r k) -> p r k", r=4),
+                    in_=w_qkv[512 * c : 512 * c + 512, :].rearrange("(r p) k -> p r k", p=P),
+                )
+            elif kind == "st":
+                j = int(tok[2])
+                for h in range(2):
+                    nc.vector.bn_stats(out=st[:, j, h, :], in_=x_sb[:, j, 512 * h : 512 * h + 512])
+                nc.vector.bn_aggr(out=mv[:, j, :], in_=st[:, j, :, :].rearrange("p a b -> p (a b)"))
+            elif kind == "sq":
+                j = int(tok[2])
+                nc.scalar.activation(out=std[:, j : j + 1], in_=mv[:, j, 1:2], func=ACT.Sqrt, bias=EPS)
+            elif kind == "rs":
+                j = int(tok[2])
+                nc.vector.reciprocal(out=rstd[:, j : j + 1], in_=std[:, j : j + 1])
+                nc.vector.tensor_scalar_mul(out=negmu[:, j : j + 1], in0=mv[:, j, 0:1], scalar1=-1.0)
+            elif kind == "xh":
+                j = int(tok[2])
+                t = xh_pool.tile([P, 8, P], F32, name="xh_t", tag="xh")
+                live["xh%d" % j] = t
+                nc.gpsimd.tensor_scalar(
+                    out=t[:].rearrange("p (gu e) q -> p gu e q", e=2),
+                    in0=x_sb[:, j, :].rearrange("p (gu q e) -> p gu e q", gu=4, e=2),
+                    scalar1=negmu[:, j : j + 1],
+                    scalar2=rstd[:, j : j + 1],
+                    op0=ALU.add,
+                    op1=ALU.mult,
+                )
+            elif kind == "tx":
+                q, g, t4 = int(tok[2]), int(tok[3]), int(tok[4])
+                t = bank(tok)
+                for jq in range(4):
+                    nc.tensor.transpose(t[:, jq, :], live["xh%d" % (4 * q + jq)][:, 4 * g + t4, :], ident[:])
+            elif kind == "ex":
+                q, g, t4 = int(tok[2]), int(tok[3]), int(tok[4])
+                pk = "pl%d%d" % (q, g)
+                if pk not in live:
+                    live[pk] = pl_pool.tile([P, 4, 512], BF16, name="planes", tag="pl")
+                gu, e = 2 * g + t4 // 2, t4 % 2
+                src = live["tx" + tok[2:5]][:].rearrange("p a b -> p (a b)")
+                if tok[5] == "v":
+                    nc.vector.tensor_scalar(
+                        out=live[pk][:, t4, :], in0=src,
+                        scalar1=wb[:, e, gu : gu + 1], scalar2=wb[:, e, 4 + gu : 5 + gu],
+                        op0=ALU.mult, op1=ALU.add,
                     )
+                else:
+                    nc.scalar.activation(
+                        out=live[pk][:, t4, :], in_=src, func=ACT.Identity,
+                        scale=wb[:, e, gu : gu + 1], bias=wb[:, e, 4 + gu : 5 + gu],
+                    )
+            elif kind == "rg":
                 gx = gx_pool.tile([P, 512, 4], BF16, name="gx", tag="gx", align_bytes=64)
+                live["gx" + tok[2:4]] = gx
                 nc.vector.tensor_copy(
                     out=gx[:].rearrange("p (c i) t -> p c t i", i=4),
-                    in_=planes[:].rearrange("p t (c i) -> p c t i", i=4),
+                    in_=live["pl" + tok[2:4]][:].rearrange("p t (c i) -> p c t i", i=4),
                 )
+            elif kind == "qx":
+                q, g = int(tok[2]), int(tok[3])
                 sl = slice((2 * q + g) * 512, (2 * q + g) * 512 + 512)
                 nc.vector.quantize_mx(
-                    out=xc[:, sl].bitcast(FP8X4),
-                    scales=xs[:, sl],
-                    in_=gx[:].rearrange("p n t -> p (n t)"),
+                    out=xc[:, sl].bitcast(FP8X4), scales=xs[:, sl],
+                    in_=live["gx" + tok[2:4]][:].rearrange("p n t -> p (n t)"),
                 )
-
-        def wprep(c, engines):
-            gw = gw_pool.tile([P, 4096], BF16, name="gw", tag="gw", align_bytes=64)
-            gwf = gw[:].bitcast(F32).rearrange("p (g n u) -> p g n u", g=2, u=2)
-            wf = wraw[c][:].bitcast(F32)
-            for r in range(4):
-                wt = tp_pool.tile([P, 4, P], F32, name="wt", tag="tp")
+            elif kind == "tw":
+                c, r = int(tok[2]), int(tok[3])
+                t = bank(tok)
+                wf = live["wraw%d" % c][:].bitcast(F32)
                 for gu in range(4):
-                    nc.tensor.transpose(wt[:, gu, :], wf[:, 512 * r + P * gu : 512 * r + P * gu + P], ident[:])
-                src = wt[:].rearrange("p (g u) f -> p g f u", u=2)
-                dst = gwf[:, :, P * r : P * r + P, :]
-                if engines[r] == "v":
-                    nc.vector.tensor_copy(out=dst, in_=src)
-                else:
-                    nc.scalar.copy(out=dst, in_=src)
-            sl = slice(c * 1024, c * 1024 + 1024)
-            nc.vector.quantize_mx(out=wc[:, sl].bitcast(FP8X4), scales=ws[:, sl], in_=gw[:])
-
-        o_tiles = {}
-
-        def mx(c, q, engines):
-            if c not in o_tiles:
-                o_tiles[c] = o_pool.tile([P, 8, NJ, 64], F32, name="o_t", tag="o")
-            o_t = o_tiles[c]
-            for jq in range(4):
-                acc = acc_pool.tile([P, 512], F32, name="acc", tag="acc")
+                    nc.tensor.transpose(t[:, gu, :], wf[:, 512 * r + P * gu : 512 * r + P * gu + P], ident[:])
+            elif kind == "ew":
+                c, r = int(tok[2]), int(tok[3])
+                gk = "gw%d" % c
+                if gk not in live:
+                    live[gk] = gw_pool.tile([P, 4096], BF16, name="gw", tag="gw", align_bytes=64)
+                gwf = live[gk][:].bitcast(F32).rearrange("p (g n u) -> p g n u", g=2, u=2)
+                copy_on(tok[4], gwf[:, :, P * r : P * r + P, :],
+                        live["tw" + tok[2:4]][:].rearrange("p (g u) f -> p g f u", u=2))
+            elif kind == "qw":
+                c = int(tok[2])
+                sl = slice(c * 1024, c * 1024 + 1024)
+                nc.vector.quantize_mx(out=wc[:, sl].bitcast(FP8X4), scales=ws[:, sl], in_=live["gw%d" % c][:])
+            elif kind == "mx":
+                c, j = int(tok[2]), int(tok[3])
+                acc = bank(tok)
                 for g in range(2):
-                    xo = (2 * q + g) * 512 + P * jq
+                    xo = (2 * (j // 4) + g) * 512 + P * (j % 4)
                     wo = c * 1024 + 512 * g
                     nc.tensor.matmul_mx(
-                        out=acc[:],
-                        lhsT=xc[:, xo : xo + P].bitcast(FP8X4),
-                        lhsT_scale=xs[:, xo : xo + P],
-                        rhs=wc[:, wo : wo + 512].bitcast(FP8X4),
-                        rhs_scale=ws[:, wo : wo + 512],
-                        start=(g == 0),
-                        stop=(g == 1),
+                        out=acc[:].rearrange("p a b -> p (a b)"),
+                        lhsT=xc[:, xo : xo + P].bitcast(FP8X4), lhsT_scale=xs[:, xo : xo + P],
+                        rhs=wc[:, wo : wo + 512].bitcast(FP8X4), rhs_scale=ws[:, wo : wo + 512],
+                        start=(g == 0), stop=(g == 1),
                     )
-                dst = o_t[:, :, 4 * q + jq, :]
-                src = acc[:].rearrange("p (h d) -> p h d", d=64)
-                if engines[jq] == "v":
-                    nc.vector.tensor_copy(out=dst, in_=src)
-                else:
-                    nc.scalar.copy(out=dst, in_=src)
-
-        def store(c, j0, j1):
-            o_t = o_tiles[c]
-            h0 = 8 * (c % 2)
-            for b in range(B):
+            elif kind == "ev":
+                c, j = int(tok[2]), int(tok[3])
+                ok = "o%d" % c
+                if ok not in live:
+                    live[ok] = o_pool.tile([P, 8, NJ, 64], F32, name="o_t", tag="o")
+                copy_on(tok[4], live[ok][:, :, j, :],
+                        live["mx" + tok[2:4]][:].rearrange("p a (x d) -> p (a x) d", d=64))
+            elif kind == "so":
+                c, j0, b = int(tok[2]), int(tok[3]), int(tok[4])
+                j1 = j0 + 4
+                h0 = 8 * (c % 2)
                 nc.sync.dma_start(
                     out=outs[c // 2][b, h0 : h0 + 8, :, :].rearrange("h (pp j) d -> pp h j d", j=NJ)[:, :, j0:j1, :],
-                    in_=o_t[b:P:4, :, j0:j1, :],
+                    in_=live["o%d" % c][b:P:4, :, j0:j1, :],
                 )
-
-        for j in range(NJ):
-            stats(j)
-            xhat(j)
-        wprep(0, "ssss")
-        xquad(0)
-        wprep(1, "ssss")
-        mx(0, 0, "sssv")
-        mx(1, 0, "sssv")
-        xquad(1)
-        wprep(2, "vvvv")
-        mx(0, 1, "sssv")
-        store(0, 0, 8)
-        mx(1, 1, "sssv")
-        store(1, 0, 8)
-        for c in range(2, NC):
-            if c + 1 < NC:
-                wprep(c + 1, "vvvv")
-            mx(c, 0, "sssv")
-            if c == NC - 1:
-                store(c, 0, 4)
-            mx(c, 1, "sssv")
-            if c == NC - 1:
-                store(c, 4, 8)
             else:
-                store(c, 0, 8)
+                assert False, tok

@@ -17,36 +17,8 @@ P = 128
 B = 4
 E = 1024
 EPS = 1e-5
-NJ = 8
-NC = 6
-
-ORDER = (
-    "ldx0b0", "ms", "warm", "ident", "ldln", "ldx0b1", "ldx0b2", "ldx0b3", "lnf", "ldx1b0", "lnT", "wb",
-    "ldx1b1", "ldx1b2", "st0", "ldx1b3", "ldw0", "st1", "sq0", "rs0", "sq1", "st2", "xh0", "ldw1",
-    "rs1", "sq2", "st3", "xh1", "tw00", "tw01", "rs2", "sq3", "st4", "xh2", "ew00s", "tw02",
-    "tw03", "ldw2", "ew01s", "rs3", "ew02s", "st5", "xh3", "sq4", "ew03s", "tw10", "tw11", "rs4",
-    "ew10s", "tw12", "st6", "xh4", "tx000", "ldw3", "sq5", "tx001", "ew11s", "tx002", "rs5", "ex000s",
-    "tx003", "st7", "xh5", "tx010", "sq6", "tx011", "ex001s", "rs6", "ex002v", "sq7", "tx012", "ex003s",
-    "ldw4", "rs7", "tx013", "ex010v", "ex011s", "tw13", "rg00", "ex012s", "ex013s", "qw0", "ldw5", "ew12s",
-    "ew13s", "rg01", "tw20", "tw21", "ew20s", "tw22", "tw23", "qx00", "xh6", "ew21s", "qx01", "ew22s",
-    "qw1", "ew23s", "xh7", "mx00", "mx01", "qw2", "ev00s", "mx02", "ev01s", "tx100", "ev02v", "tx101",
-    "ex100s", "tx102", "ex101v", "tx103", "tx110", "ex102s", "ex103v", "tx111", "tx112", "ex110s", "ex111v", "tx113",
-    "mx03", "ex112s", "rg10", "mx10", "ex113s", "mx11", "ev03v", "ev10s", "mx12", "rg11", "ev11s", "so000",
-    "mx13", "ev12s", "so001", "mx20", "qx10", "ev13s", "mx21", "so002", "ev20s", "qx11", "mx22", "so003",
-    "ev21s", "mx23", "so100", "ev22v", "mx04", "ev23s", "so101", "mx05", "ev04v", "so102", "mx06", "ev05s",
-    "mx07", "so103", "ev06v", "mx14", "so200", "ev07s", "mx15", "so201", "ev14v", "mx16", "ev15s", "so040",
-    "mx17", "ev16v", "so041", "tw30", "ev17s", "tw31", "so042", "ew30v", "tw32", "ew31s", "tw33", "so043",
-    "ew32v", "mx24", "ew33s", "so140", "mx25", "qw3", "ev24s", "mx26", "so141", "ev25s", "mx27", "so142",
-    "ev26s", "tw40", "so143", "ev27v", "tw41", "ew40s", "tw42", "so202", "ew41v", "tw43", "ew42s", "mx30",
-    "so203", "ew43v", "mx31", "so240", "ev30v", "mx32", "ev31s", "qw4", "so241", "mx33", "ev32s", "so242",
-    "mx34", "ev33s", "mx35", "so243", "ev34v", "mx36", "so300", "ev35s", "mx37", "so301", "ev36v", "mx40",
-    "ev37s", "so302", "mx41", "ev40v", "so303", "mx42", "ev41s", "mx43", "so340", "ev42v", "tw50", "so341",
-    "ev43s", "tw51", "ew50v", "tw52", "so342", "ew51s", "tw53", "ew52v", "mx44", "so343", "ew53s", "mx45",
-    "so400", "qw5", "ev44s", "mx46", "so401", "ev45s", "mx47", "ev46s", "so402", "mx50", "ev47v", "so403",
-    "mx51", "ev50v", "so440", "mx52", "ev51s", "so441", "mx53", "ev52v", "mx54", "so442", "ev53s", "mx55",
-    "so443", "ev54v", "mx56", "ev55s", "so500", "mx57", "ev56v", "so501", "ev57s", "so502", "so503", "so540",
-    "so541", "so542", "so543",
-)
+TILES = 8
+CHUNKS = 6
 
 
 def tile_selfattention_pa_kernel(tc, inputs, ln_w, ln_b, w_qkv, out_0, out_1, out_2):
@@ -54,12 +26,12 @@ def tile_selfattention_pa_kernel(tc, inputs, ln_w, ln_b, w_qkv, out_0, out_1, ou
     outs = (out_0, out_1, out_2)
     with ExitStack() as ctx:
         const = ctx.enter_context(tc.tile_pool(name="const", bufs=1))
-        wraw_pool = ctx.enter_context(tc.tile_pool(name="wraw", bufs=NC))
+        wraw_pool = ctx.enter_context(tc.tile_pool(name="wraw", bufs=CHUNKS))
         gw_pool = ctx.enter_context(tc.tile_pool(name="gw", bufs=2))
-        xh_pool = ctx.enter_context(tc.tile_pool(name="xh", bufs=6))
-        pl_pool = ctx.enter_context(tc.tile_pool(name="pl", bufs=3))
-        gx_pool = ctx.enter_context(tc.tile_pool(name="gx", bufs=3))
-        o_pool = ctx.enter_context(tc.tile_pool(name="o", bufs=3))
+        xh_pool = ctx.enter_context(tc.tile_pool(name="xh", bufs=8))
+        pl_pool = ctx.enter_context(tc.tile_pool(name="pl", bufs=2))
+        gx_pool = ctx.enter_context(tc.tile_pool(name="gx", bufs=2))
+        o_pool = ctx.enter_context(tc.tile_pool(name="o", bufs=6))
         ps_pool = ctx.enter_context(tc.psum_pool(name="ps", bufs=8))
         ctx.enter_context(tc.manual_schedule())
 
@@ -69,17 +41,18 @@ def tile_selfattention_pa_kernel(tc, inputs, ln_w, ln_b, w_qkv, out_0, out_1, ou
         lnrow = const.tile([P, 256], BF16)
         lnf = const.tile([P, 2, P], F32)
         wb = const.tile([P, 2, 8], F32)
-        x_sb = const.tile([P, NJ, E], BF16)
+        x_sb = {}
         xc = const.tile([P, 2 * 2 * 512], U32, align_bytes=64)
         xs = const.tile([P, 2 * 2 * 512], U8, align_bytes=64)
-        wc = const.tile([P, NC * 1024], U32, align_bytes=64)
-        ws = const.tile([P, NC * 1024], U8, align_bytes=64)
-        st = const.tile([P, NJ, 2, 6], F32)
-        mv = const.tile([P, NJ, 2], F32)
-        std = const.tile([P, NJ], F32)
-        rstd = const.tile([P, NJ], F32)
-        negmu = const.tile([P, NJ], F32)
-        live = {}
+        wc = const.tile([P, CHUNKS * 1024], U32, align_bytes=64)
+        ws = const.tile([P, CHUNKS * 1024], U8, align_bytes=64)
+        st = const.tile([P, TILES, 2, 6], F32)
+        mv = const.tile([P, TILES, 2], F32)
+        std = const.tile([P, TILES], F32)
+        rstd = const.tile([P, TILES], F32)
+        negmu = const.tile([P, TILES], F32)
+        wraw = []
+        xh = {}
 
         def copy_on(eng, dst, src):
             if eng == "v":
@@ -87,130 +60,119 @@ def tile_selfattention_pa_kernel(tc, inputs, ln_w, ln_b, w_qkv, out_0, out_1, ou
             else:
                 nc.scalar.copy(out=dst, in_=src)
 
-        def bank(key):
-            t = ps_pool.tile([P, 4, P], F32, name="bank", tag="ps")
-            live[key] = t
+        def bank():
+            return ps_pool.tile([P, 4, P], F32, name="bank", tag="ps")
+
+        def load_x(j0, j1):
+            x_t = const.tile([P, j1 - j0, E], BF16, name="x_t%d" % j0)
+            for b in range(B):
+                nc.sync.dma_start(
+                    out=x_t[b:P:4, :, :],
+                    in_=inputs[b].rearrange("(pp j) k -> pp j k", j=TILES)[:, j0:j1, :],
+                )
+            for j in range(j0, j1):
+                x_sb[j] = x_t[:, j - j0, :]
+
+        def load_w(c):
+            w_t = wraw_pool.tile([P, 4 * E], BF16, name="wraw_t", tag="wraw")
+            nc.sync.dma_start(
+                out=w_t[:].rearrange("p (r k) -> p r k", r=4),
+                in_=w_qkv[512 * c : 512 * c + 512, :].rearrange("(r p) k -> p r k", p=P),
+            )
+            wraw.append(w_t)
+
+        def statistics(j):
+            for h in range(2):
+                nc.vector.bn_stats(out=st[:, j, h, :], in_=x_sb[j][:, 512 * h : 512 * h + 512])
+            nc.vector.bn_aggr(out=mv[:, j, :], in_=st[:, j, :, :].rearrange("p a b -> p (a b)"))
+            nc.scalar.activation(out=std[:, j : j + 1], in_=mv[:, j, 1:2], func=ACT.Sqrt, bias=EPS)
+
+        def normalise(j):
+            nc.vector.reciprocal(out=rstd[:, j : j + 1], in_=std[:, j : j + 1])
+            nc.vector.tensor_scalar_mul(out=negmu[:, j : j + 1], in0=mv[:, j, 0:1], scalar1=-1.0)
+            t = xh_pool.tile([P, 8, P], F32, name="xh_t", tag="xh")
+            nc.gpsimd.tensor_scalar(
+                out=t[:].rearrange("p (gu e) q -> p gu e q", e=2),
+                in0=x_sb[j].rearrange("p (gu q e) -> p gu e q", gu=4, e=2),
+                scalar1=negmu[:, j : j + 1],
+                scalar2=rstd[:, j : j + 1],
+                op0=ALU.add,
+                op1=ALU.mult,
+            )
+            xh[j] = t
+
+        gw = {}
+
+        def w_transposes(c, r):
+            t = bank()
+            wf = wraw[c][:].bitcast(F32)
+            for gu in range(4):
+                nc.tensor.transpose(t[:, gu, :], wf[:, 512 * r + P * gu : 512 * r + P * gu + P], ident[:])
             return t
 
-        for tok in ORDER:
-            kind = tok[0:2]
-            if tok == "ident":
-                make_identity(nc, ident[:])
-            elif tok == "ms":
-                nc.vector.memset(one[:], 1.0)
-                nc.vector.memset(lnrow[:], 0.0)
-            elif tok == "warm":
-                nc.scalar.activation(out=warm[:], in_=one[:], func=ACT.Sqrt)
-            elif tok == "ldln":
-                nc.scalar.dma_start(out=lnrow[0:4, :], in_=ln_w.rearrange("(r c) -> r c", c=256))
-                nc.scalar.dma_start(out=lnrow[4:8, :], in_=ln_b.rearrange("(r c) -> r c", c=256))
-            elif tok == "lnf":
-                nc.vector.tensor_copy(out=lnf[:], in_=lnrow[:].rearrange("p (q e) -> p e q", e=2))
-            elif tok == "lnT":
-                t = bank("ln")
-                for e in range(2):
-                    nc.tensor.transpose(t[:, e, :], lnf[:, e, :], ident[:])
-            elif tok == "wb":
-                nc.vector.tensor_copy(out=wb[:], in_=live["ln"][:, 0:2, 0:8])
-            elif tok[0:3] == "ldx":
-                q, b = int(tok[3]), int(tok[5])
-                js = slice(4 * q, 4 * q + 4)
-                nc.sync.dma_start(
-                    out=x_sb[b:P:4, js, :],
-                    in_=inputs[b].rearrange("(pp j) k -> pp j k", j=NJ)[:, js, :],
-                )
-            elif tok[0:3] == "ldw":
-                c = int(tok[3])
-                w_t = wraw_pool.tile([P, 4 * E], BF16, name="wraw_t", tag="wraw")
-                live["wraw%d" % c] = w_t
-                nc.sync.dma_start(
-                    out=w_t[:].rearrange("p (r k) -> p r k", r=4),
-                    in_=w_qkv[512 * c : 512 * c + 512, :].rearrange("(r p) k -> p r k", p=P),
-                )
-            elif kind == "st":
-                j = int(tok[2])
-                for h in range(2):
-                    nc.vector.bn_stats(out=st[:, j, h, :], in_=x_sb[:, j, 512 * h : 512 * h + 512])
-                nc.vector.bn_aggr(out=mv[:, j, :], in_=st[:, j, :, :].rearrange("p a b -> p (a b)"))
-            elif kind == "sq":
-                j = int(tok[2])
-                nc.scalar.activation(out=std[:, j : j + 1], in_=mv[:, j, 1:2], func=ACT.Sqrt, bias=EPS)
-            elif kind == "rs":
-                j = int(tok[2])
-                nc.vector.reciprocal(out=rstd[:, j : j + 1], in_=std[:, j : j + 1])
-                nc.vector.tensor_scalar_mul(out=negmu[:, j : j + 1], in0=mv[:, j, 0:1], scalar1=-1.0)
-            elif kind == "xh":
-                j = int(tok[2])
-                t = xh_pool.tile([P, 8, P], F32, name="xh_t", tag="xh")
-                live["xh%d" % j] = t
-                nc.gpsimd.tensor_scalar(
-                    out=t[:].rearrange("p (gu e) q -> p gu e q", e=2),
-                    in0=x_sb[:, j, :].rearrange("p (gu q e) -> p gu e q", gu=4, e=2),
-                    scalar1=negmu[:, j : j + 1],
-                    scalar2=rstd[:, j : j + 1],
-                    op0=ALU.add,
-                    op1=ALU.mult,
-                )
-            elif kind == "tx":
-                q, g, t4 = int(tok[2]), int(tok[3]), int(tok[4])
-                t = bank(tok)
+        def w_copy(c, r, t, eng):
+            if c not in gw:
+                gw[c] = gw_pool.tile([P, 4096], BF16, name="gw_t", tag="gw", align_bytes=64)
+            gwf = gw[c][:].bitcast(F32).rearrange("p (g n u) -> p g n u", g=2, u=2)
+            copy_on(eng, gwf[:, :, P * r : P * r + P, :], t[:].rearrange("p (g u) f -> p g f u", u=2))
+
+        def w_quantise(c):
+            sl = slice(c * 1024, c * 1024 + 1024)
+            nc.vector.quantize_mx(out=wc[:, sl].bitcast(FP8X4), scales=ws[:, sl], in_=gw[c][:])
+
+        def prepare_w(c, engines):
+            banks = [w_transposes(c, r) for r in range(4)]
+            for r in range(4):
+                w_copy(c, r, banks[r], engines[r])
+            w_quantise(c)
+
+        def x_regroup(planes):
+            gx = gx_pool.tile([P, 512, 4], BF16, name="gx_t", tag="gx", align_bytes=64)
+            nc.vector.tensor_copy(
+                out=gx[:].rearrange("p (c i) t -> p c t i", i=4),
+                in_=planes[:].rearrange("p t (c i) -> p c t i", i=4),
+            )
+            return gx
+
+        def x_quantise(q, g, gx):
+            sl = slice((2 * q + g) * 512, (2 * q + g) * 512 + 512)
+            nc.vector.quantize_mx(out=xc[:, sl].bitcast(FP8X4), scales=xs[:, sl], in_=gx[:].rearrange("p n t -> p (n t)"))
+
+        def prepare_x(q, between):
+            planes = [pl_pool.tile([P, 4, 512], BF16, name="planes", tag="pl") for g in range(2)]
+            gx = [None, None]
+            for t in range(8):
+                g, t4 = t // 4, t % 4
+                gu, e = t // 2, t % 2
+                xt = bank()
                 for jq in range(4):
-                    nc.tensor.transpose(t[:, jq, :], live["xh%d" % (4 * q + jq)][:, 4 * g + t4, :], ident[:])
-            elif kind == "ex":
-                q, g, t4 = int(tok[2]), int(tok[3]), int(tok[4])
-                pk = "pl%d%d" % (q, g)
-                if pk not in live:
-                    live[pk] = pl_pool.tile([P, 4, 512], BF16, name="planes", tag="pl")
-                gu, e = 2 * g + t4 // 2, t4 % 2
-                src = live["tx" + tok[2:5]][:].rearrange("p a b -> p (a b)")
-                if tok[5] == "v":
+                    nc.tensor.transpose(xt[:, jq, :], xh[4 * q + jq][:, t, :], ident[:])
+                src = xt[:].rearrange("p a b -> p (a b)")
+                if t % 2 == 1:
                     nc.vector.tensor_scalar(
-                        out=live[pk][:, t4, :], in0=src,
+                        out=planes[g][:, t4, :], in0=src,
                         scalar1=wb[:, e, gu : gu + 1], scalar2=wb[:, e, 4 + gu : 5 + gu],
                         op0=ALU.mult, op1=ALU.add,
                     )
                 else:
                     nc.scalar.activation(
-                        out=live[pk][:, t4, :], in_=src, func=ACT.Identity,
+                        out=planes[g][:, t4, :], in_=src, func=ACT.Identity,
                         scale=wb[:, e, gu : gu + 1], bias=wb[:, e, 4 + gu : 5 + gu],
                     )
-            elif kind == "rg":
-                gx = gx_pool.tile([P, 512, 4], BF16, name="gx", tag="gx", align_bytes=64)
-                live["gx" + tok[2:4]] = gx
-                nc.vector.tensor_copy(
-                    out=gx[:].rearrange("p (c i) t -> p c t i", i=4),
-                    in_=live["pl" + tok[2:4]][:].rearrange("p t (c i) -> p c t i", i=4),
-                )
-            elif kind == "qx":
-                q, g = int(tok[2]), int(tok[3])
-                sl = slice((2 * q + g) * 512, (2 * q + g) * 512 + 512)
-                nc.vector.quantize_mx(
-                    out=xc[:, sl].bitcast(FP8X4), scales=xs[:, sl],
-                    in_=live["gx" + tok[2:4]][:].rearrange("p n t -> p (n t)"),
-                )
-            elif kind == "tw":
-                c, r = int(tok[2]), int(tok[3])
-                t = bank(tok)
-                wf = live["wraw%d" % c][:].bitcast(F32)
-                for gu in range(4):
-                    nc.tensor.transpose(t[:, gu, :], wf[:, 512 * r + P * gu : 512 * r + P * gu + P], ident[:])
-            elif kind == "ew":
-                c, r = int(tok[2]), int(tok[3])
-                gk = "gw%d" % c
-                if gk not in live:
-                    live[gk] = gw_pool.tile([P, 4096], BF16, name="gw", tag="gw", align_bytes=64)
-                gwf = live[gk][:].bitcast(F32).rearrange("p (g n u) -> p g n u", g=2, u=2)
-                copy_on(tok[4], gwf[:, :, P * r : P * r + P, :],
-                        live["tw" + tok[2:4]][:].rearrange("p (g u) f -> p g f u", u=2))
-            elif kind == "qw":
-                c = int(tok[2])
-                sl = slice(c * 1024, c * 1024 + 1024)
-                nc.vector.quantize_mx(out=wc[:, sl].bitcast(FP8X4), scales=ws[:, sl], in_=live["gw%d" % c][:])
-            elif kind == "mx":
-                c, j = int(tok[2]), int(tok[3])
-                acc = bank(tok)
+                if t == 3 and between is not None:
+                    between()
+                if t == 5:
+                    gx[0] = x_regroup(planes[0])
+            gx[1] = x_regroup(planes[1])
+            x_quantise(q, 0, gx[0])
+            x_quantise(q, 1, gx[1])
+
+        def project(c, q, engines):
+            accs = []
+            for jq in range(4):
+                acc = bank()
                 for g in range(2):
-                    xo = (2 * (j // 4) + g) * 512 + P * (j % 4)
+                    xo = (2 * q + g) * 512 + P * jq
                     wo = c * 1024 + 512 * g
                     nc.tensor.matmul_mx(
                         out=acc[:].rearrange("p a b -> p (a b)"),
@@ -218,20 +180,61 @@ def tile_selfattention_pa_kernel(tc, inputs, ln_w, ln_b, w_qkv, out_0, out_1, ou
                         rhs=wc[:, wo : wo + 512].bitcast(FP8X4), rhs_scale=ws[:, wo : wo + 512],
                         start=(g == 0), stop=(g == 1),
                     )
-            elif kind == "ev":
-                c, j = int(tok[2]), int(tok[3])
-                ok = "o%d" % c
-                if ok not in live:
-                    live[ok] = o_pool.tile([P, 8, NJ, 64], F32, name="o_t", tag="o")
-                copy_on(tok[4], live[ok][:, :, j, :],
-                        live["mx" + tok[2:4]][:].rearrange("p a (x d) -> p (a x) d", d=64))
-            elif kind == "so":
-                c, j0, b = int(tok[2]), int(tok[3]), int(tok[4])
-                j1 = j0 + 4
-                h0 = 8 * (c % 2)
+                accs.append(acc)
+            o_t = o_pool.tile([P, 8, 4, 64], F32, name="o_t", tag="o")
+            for jq in range(4):
+                copy_on(engines[jq], o_t[:, :, jq, :], accs[jq][:].rearrange("p a (x d) -> p (a x) d", d=64))
+            h0 = 8 * (c % 2)
+            for b in range(B):
                 nc.sync.dma_start(
-                    out=outs[c // 2][b, h0 : h0 + 8, :, :].rearrange("h (pp j) d -> pp h j d", j=NJ)[:, :, j0:j1, :],
-                    in_=live["o%d" % c][b:P:4, :, j0:j1, :],
+                    out=outs[c // 2][b, h0 : h0 + 8, :, :].rearrange("h (pp j) d -> pp h j d", j=TILES)[:, :, 4 * q : 4 * q + 4, :],
+                    in_=o_t[b:P:4, :, :, :],
                 )
-            else:
-                assert False, tok
+
+        nc.vector.memset(lnrow[:], 0.0)
+        nc.scalar.dma_start(out=lnrow[0:4, :], in_=ln_w.rearrange("(r c) -> r c", c=256))
+        nc.scalar.dma_start(out=lnrow[4:8, :], in_=ln_b.rearrange("(r c) -> r c", c=256))
+        load_x(0, 1)
+        load_x(1, 2)
+        load_x(2, 4)
+        load_w(0)
+        load_x(4, 8)
+        for c in range(1, CHUNKS):
+            load_w(c)
+        make_identity(nc, ident[:])
+        nc.vector.memset(one[:], 1.0)
+        nc.scalar.activation(out=warm[:], in_=one[:], func=ACT.Sqrt)
+
+        for k in range(TILES + 1):
+            if k < TILES:
+                statistics(k)
+            if k >= 1:
+                normalise(k - 1)
+            if k == 1:
+                nc.vector.tensor_copy(out=lnf[:], in_=lnrow[:].rearrange("p (q e) -> p e q", e=2))
+                lnt = bank()
+                for e in range(2):
+                    nc.tensor.transpose(lnt[:, e, :], lnf[:, e, :], ident[:])
+            if k == 2:
+                nc.vector.tensor_copy(out=wb[:], in_=lnt[:, 0:2, 0:8])
+            if k in (3, 4):
+                for r in (2 * (k - 3), 2 * (k - 3) + 1):
+                    w_copy(0, r, w_transposes(0, r), "s")
+
+        prepare_x(0, lambda: w_quantise(0))
+        prepare_w(1, "ssss")
+        prepare_w(2, "ssss")
+        project(0, 0, "sssv")
+        prepare_x(1, None)
+        project(1, 0, "sssv")
+        project(2, 0, "sssv")
+        project(0, 1, "svsv")
+        project(1, 1, "svsv")
+        prepare_w(3, "svsv")
+        project(2, 1, "svsv")
+        prepare_w(4, "svsv")
+        for c in range(3, CHUNKS):
+            project(c, 0, "svsv")
+            if c == 3:
+                prepare_w(5, "svsv")
+            project(c, 1, "svsv")

@@ -81,10 +81,13 @@ def tile_selfattention_pa_kernel(tc, inputs, ln_w, ln_b, w_qkv, out_0, out_1, ou
             )
             wraw.append(w_t)
 
-        def statistics(j):
-            for h in range(2):
-                nc.vector.bn_stats(out=st[:, j, h, :], in_=x_sb[j][:, 512 * h : 512 * h + 512])
+        def half_statistics(j, h):
+            nc.vector.bn_stats(out=st[:, j, h, :], in_=x_sb[j][:, 512 * h : 512 * h + 512])
+
+        def mean_and_variance(j):
             nc.vector.bn_aggr(out=mv[:, j, :], in_=st[:, j, :, :].rearrange("p a b -> p (a b)"))
+
+        def standard_deviation(j):
             nc.scalar.activation(out=std[:, j : j + 1], in_=mv[:, j, 1:2], func=ACT.Sqrt, bias=EPS)
 
         def normalise(j):
@@ -138,7 +141,16 @@ def tile_selfattention_pa_kernel(tc, inputs, ln_w, ln_b, w_qkv, out_0, out_1, ou
             sl = slice((2 * q + g) * 512, (2 * q + g) * 512 + 512)
             nc.vector.quantize_mx(out=xc[:, sl].bitcast(FP8X4), scales=xs[:, sl], in_=gx[:].rearrange("p n t -> p (n t)"))
 
-        def prepare_x(q, between):
+        def layer_norm_step(k):
+            if k < TILES:
+                half_statistics(k, 0)
+            if k >= 1:
+                normalise(k - 1)
+            if k < TILES:
+                half_statistics(k, 1)
+                mean_and_variance(k)
+
+        def prepare_x(q, engines, fillers):
             planes = [pl_pool.tile([P, 4, 512], BF16, name="planes", tag="pl") for g in range(2)]
             gx = [None, None]
             for t in range(8):
@@ -148,7 +160,7 @@ def tile_selfattention_pa_kernel(tc, inputs, ln_w, ln_b, w_qkv, out_0, out_1, ou
                 for jq in range(4):
                     nc.tensor.transpose(xt[:, jq, :], xh[4 * q + jq][:, t, :], ident[:])
                 src = xt[:].rearrange("p a b -> p (a b)")
-                if t % 2 == 1:
+                if engines[t] == "v":
                     nc.vector.tensor_scalar(
                         out=planes[g][:, t4, :], in0=src,
                         scalar1=wb[:, e, gu : gu + 1], scalar2=wb[:, e, 4 + gu : 5 + gu],
@@ -159,12 +171,13 @@ def tile_selfattention_pa_kernel(tc, inputs, ln_w, ln_b, w_qkv, out_0, out_1, ou
                         out=planes[g][:, t4, :], in_=src, func=ACT.Identity,
                         scale=wb[:, e, gu : gu + 1], bias=wb[:, e, 4 + gu : 5 + gu],
                     )
-                if t == 3 and between is not None:
-                    between()
-                if t == 5:
+                if t == 3:
                     gx[0] = x_regroup(planes[0])
-            gx[1] = x_regroup(planes[1])
+                    fillers[0]()
+            fillers[1]()
             x_quantise(q, 0, gx[0])
+            gx[1] = x_regroup(planes[1])
+            fillers[2]()
             x_quantise(q, 1, gx[1])
 
         def project(c, q, engines):
@@ -205,11 +218,9 @@ def tile_selfattention_pa_kernel(tc, inputs, ln_w, ln_b, w_qkv, out_0, out_1, ou
         nc.vector.memset(one[:], 1.0)
         nc.scalar.activation(out=warm[:], in_=one[:], func=ACT.Sqrt)
 
-        for k in range(TILES + 1):
-            if k < TILES:
-                statistics(k)
-            if k >= 1:
-                normalise(k - 1)
+        for k in range(TILES - 1):
+            layer_norm_step(k)
+            standard_deviation(k)
             if k == 1:
                 nc.vector.tensor_copy(out=lnf[:], in_=lnrow[:].rearrange("p (q e) -> p e q", e=2))
                 lnt = bank()
@@ -220,12 +231,18 @@ def tile_selfattention_pa_kernel(tc, inputs, ln_w, ln_b, w_qkv, out_0, out_1, ou
             if k in (3, 4):
                 for r in (2 * (k - 3), 2 * (k - 3) + 1):
                     w_copy(0, r, w_transposes(0, r), "s")
+            if k == 5:
+                w_quantise(0)
 
-        prepare_x(0, lambda: w_quantise(0))
+        prepare_x(
+            0,
+            "ssssssss",
+            (lambda: layer_norm_step(TILES - 1), lambda: standard_deviation(TILES - 1), lambda: layer_norm_step(TILES)),
+        )
         prepare_w(1, "ssss")
         prepare_w(2, "ssss")
         project(0, 0, "sssv")
-        prepare_x(1, None)
+        prepare_x(1, "svsvsvsv", (lambda: None, lambda: None, lambda: None))
         project(1, 0, "sssv")
         project(2, 0, "sssv")
         project(0, 1, "svsv")

@@ -28,10 +28,11 @@ def tile_selfattention_pa_kernel(tc, inputs, ln_w, ln_b, w_qkv, out_0, out_1, ou
         const = ctx.enter_context(tc.tile_pool(name="const", bufs=1))
         wraw_pool = ctx.enter_context(tc.tile_pool(name="wraw", bufs=CHUNKS))
         gw_pool = ctx.enter_context(tc.tile_pool(name="gw", bufs=2))
-        xh_pool = ctx.enter_context(tc.tile_pool(name="xh", bufs=8))
+        xh_pool = ctx.enter_context(tc.tile_pool(name="xh", bufs=6))
         pl_pool = ctx.enter_context(tc.tile_pool(name="pl", bufs=2))
         gx_pool = ctx.enter_context(tc.tile_pool(name="gx", bufs=2))
-        o_pool = ctx.enter_context(tc.tile_pool(name="o", bufs=6))
+        o_pool = ctx.enter_context(tc.tile_pool(name="o", bufs=4))
+        o8_pool = ctx.enter_context(tc.tile_pool(name="o8", bufs=2))
         ps_pool = ctx.enter_context(tc.psum_pool(name="ps", bufs=8))
         ctx.enter_context(tc.manual_schedule())
 
@@ -81,13 +82,10 @@ def tile_selfattention_pa_kernel(tc, inputs, ln_w, ln_b, w_qkv, out_0, out_1, ou
             )
             wraw.append(w_t)
 
-        def half_statistics(j, h):
-            nc.vector.bn_stats(out=st[:, j, h, :], in_=x_sb[j][:, 512 * h : 512 * h + 512])
-
-        def mean_and_variance(j):
+        def statistics(j):
+            for h in range(2):
+                nc.vector.bn_stats(out=st[:, j, h, :], in_=x_sb[j][:, 512 * h : 512 * h + 512])
             nc.vector.bn_aggr(out=mv[:, j, :], in_=st[:, j, :, :].rearrange("p a b -> p (a b)"))
-
-        def standard_deviation(j):
             nc.scalar.activation(out=std[:, j : j + 1], in_=mv[:, j, 1:2], func=ACT.Sqrt, bias=EPS)
 
         def normalise(j):
@@ -141,16 +139,7 @@ def tile_selfattention_pa_kernel(tc, inputs, ln_w, ln_b, w_qkv, out_0, out_1, ou
             sl = slice((2 * q + g) * 512, (2 * q + g) * 512 + 512)
             nc.vector.quantize_mx(out=xc[:, sl].bitcast(FP8X4), scales=xs[:, sl], in_=gx[:].rearrange("p n t -> p (n t)"))
 
-        def layer_norm_step(k):
-            if k < TILES:
-                half_statistics(k, 0)
-            if k >= 1:
-                normalise(k - 1)
-            if k < TILES:
-                half_statistics(k, 1)
-                mean_and_variance(k)
-
-        def prepare_x(q, engines, fillers):
+        def prepare_x(q, between):
             planes = [pl_pool.tile([P, 4, 512], BF16, name="planes", tag="pl") for g in range(2)]
             gx = [None, None]
             for t in range(8):
@@ -160,7 +149,7 @@ def tile_selfattention_pa_kernel(tc, inputs, ln_w, ln_b, w_qkv, out_0, out_1, ou
                 for jq in range(4):
                     nc.tensor.transpose(xt[:, jq, :], xh[4 * q + jq][:, t, :], ident[:])
                 src = xt[:].rearrange("p a b -> p (a b)")
-                if engines[t] == "v":
+                if t % 2 == 1:
                     nc.vector.tensor_scalar(
                         out=planes[g][:, t4, :], in0=src,
                         scalar1=wb[:, e, gu : gu + 1], scalar2=wb[:, e, 4 + gu : 5 + gu],
@@ -171,16 +160,15 @@ def tile_selfattention_pa_kernel(tc, inputs, ln_w, ln_b, w_qkv, out_0, out_1, ou
                         out=planes[g][:, t4, :], in_=src, func=ACT.Identity,
                         scale=wb[:, e, gu : gu + 1], bias=wb[:, e, 4 + gu : 5 + gu],
                     )
-                if t == 3:
+                if t == 3 and between is not None:
+                    between()
+                if t == 5:
                     gx[0] = x_regroup(planes[0])
-                    fillers[0]()
-            fillers[1]()
-            x_quantise(q, 0, gx[0])
             gx[1] = x_regroup(planes[1])
-            fillers[2]()
+            x_quantise(q, 0, gx[0])
             x_quantise(q, 1, gx[1])
 
-        def project(c, q, engines):
+        def project(c, q, engines, o_t, j0):
             accs = []
             for jq in range(4):
                 acc = bank()
@@ -194,15 +182,21 @@ def tile_selfattention_pa_kernel(tc, inputs, ln_w, ln_b, w_qkv, out_0, out_1, ou
                         start=(g == 0), stop=(g == 1),
                     )
                 accs.append(acc)
-            o_t = o_pool.tile([P, 8, 4, 64], F32, name="o_t", tag="o")
             for jq in range(4):
-                copy_on(engines[jq], o_t[:, :, jq, :], accs[jq][:].rearrange("p a (x d) -> p (a x) d", d=64))
+                copy_on(engines[jq], o_t[:, :, j0 + jq, :], accs[jq][:].rearrange("p a (x d) -> p (a x) d", d=64))
+
+        def store(c, o_t, first, count):
             h0 = 8 * (c % 2)
             for b in range(B):
                 nc.sync.dma_start(
-                    out=outs[c // 2][b, h0 : h0 + 8, :, :].rearrange("h (pp j) d -> pp h j d", j=TILES)[:, :, 4 * q : 4 * q + 4, :],
+                    out=outs[c // 2][b, h0 : h0 + 8, :, :].rearrange("h (pp j) d -> pp h j d", j=TILES)[:, :, first : first + count, :],
                     in_=o_t[b:P:4, :, :, :],
                 )
+
+        def project_quad(c, q, engines):
+            o_t = o_pool.tile([P, 8, 4, 64], F32, name="o_t", tag="o")
+            project(c, q, engines, o_t, 0)
+            store(c, o_t, 4 * q, 4)
 
         nc.vector.memset(lnrow[:], 0.0)
         nc.scalar.dma_start(out=lnrow[0:4, :], in_=ln_w.rearrange("(r c) -> r c", c=256))
@@ -218,9 +212,11 @@ def tile_selfattention_pa_kernel(tc, inputs, ln_w, ln_b, w_qkv, out_0, out_1, ou
         nc.vector.memset(one[:], 1.0)
         nc.scalar.activation(out=warm[:], in_=one[:], func=ACT.Sqrt)
 
-        for k in range(TILES - 1):
-            layer_norm_step(k)
-            standard_deviation(k)
+        for k in range(TILES + 1):
+            if k < TILES:
+                statistics(k)
+            if k >= 1:
+                normalise(k - 1)
             if k == 1:
                 nc.vector.tensor_copy(out=lnf[:], in_=lnrow[:].rearrange("p (q e) -> p e q", e=2))
                 lnt = bank()
@@ -231,27 +227,25 @@ def tile_selfattention_pa_kernel(tc, inputs, ln_w, ln_b, w_qkv, out_0, out_1, ou
             if k in (3, 4):
                 for r in (2 * (k - 3), 2 * (k - 3) + 1):
                     w_copy(0, r, w_transposes(0, r), "s")
-            if k == 5:
-                w_quantise(0)
 
-        prepare_x(
-            0,
-            "ssssssss",
-            (lambda: layer_norm_step(TILES - 1), lambda: standard_deviation(TILES - 1), lambda: layer_norm_step(TILES)),
-        )
+        prepare_x(0, lambda: w_quantise(0))
         prepare_w(1, "ssss")
         prepare_w(2, "ssss")
-        project(0, 0, "sssv")
-        prepare_x(1, "svsvsvsv", (lambda: None, lambda: None, lambda: None))
-        project(1, 0, "sssv")
-        project(2, 0, "sssv")
-        project(0, 1, "svsv")
-        project(1, 1, "svsv")
+        project_quad(0, 0, "sssv")
+        prepare_x(1, None)
+        project_quad(1, 0, "sssv")
+        project_quad(2, 0, "sssv")
+        project_quad(0, 1, "svsv")
+        project_quad(1, 1, "svsv")
         prepare_w(3, "svsv")
-        project(2, 1, "svsv")
+        project_quad(2, 1, "svsv")
         prepare_w(4, "svsv")
-        for c in range(3, CHUNKS):
-            project(c, 0, "svsv")
+        for c in (3, 4):
+            o_t = o8_pool.tile([P, 8, TILES, 64], F32, name="o8_t", tag="o8")
+            project(c, 0, "svsv", o_t, 0)
             if c == 3:
                 prepare_w(5, "svsv")
-            project(c, 1, "svsv")
+            project(c, 1, "svsv", o_t, 4)
+            store(c, o_t, 0, TILES)
+        project_quad(5, 0, "svsv")
+        project_quad(5, 1, "svsv")

@@ -28,11 +28,10 @@ def tile_selfattention_pa_kernel(tc, inputs, ln_w, ln_b, w_qkv, out_0, out_1, ou
         const = ctx.enter_context(tc.tile_pool(name="const", bufs=1))
         wraw_pool = ctx.enter_context(tc.tile_pool(name="wraw", bufs=CHUNKS))
         gw_pool = ctx.enter_context(tc.tile_pool(name="gw", bufs=2))
-        xh_pool = ctx.enter_context(tc.tile_pool(name="xh", bufs=6))
+        xh_pool = ctx.enter_context(tc.tile_pool(name="xh", bufs=8))
         pl_pool = ctx.enter_context(tc.tile_pool(name="pl", bufs=2))
         gx_pool = ctx.enter_context(tc.tile_pool(name="gx", bufs=2))
-        o_pool = ctx.enter_context(tc.tile_pool(name="o", bufs=4))
-        o8_pool = ctx.enter_context(tc.tile_pool(name="o8", bufs=2))
+        o_pool = ctx.enter_context(tc.tile_pool(name="o", bufs=6))
         ps_pool = ctx.enter_context(tc.psum_pool(name="ps", bufs=8))
         ctx.enter_context(tc.manual_schedule())
 
@@ -168,7 +167,7 @@ def tile_selfattention_pa_kernel(tc, inputs, ln_w, ln_b, w_qkv, out_0, out_1, ou
             x_quantise(q, 0, gx[0])
             x_quantise(q, 1, gx[1])
 
-        def project(c, q, engines, o_t, j0):
+        def project(c, q, engines):
             accs = []
             for jq in range(4):
                 acc = bank()
@@ -182,21 +181,16 @@ def tile_selfattention_pa_kernel(tc, inputs, ln_w, ln_b, w_qkv, out_0, out_1, ou
                         start=(g == 0), stop=(g == 1),
                     )
                 accs.append(acc)
-            for jq in range(4):
-                copy_on(engines[jq], o_t[:, :, j0 + jq, :], accs[jq][:].rearrange("p a (x d) -> p (a x) d", d=64))
-
-        def store(c, o_t, first, count):
-            h0 = 8 * (c % 2)
-            for b in range(B):
-                nc.sync.dma_start(
-                    out=outs[c // 2][b, h0 : h0 + 8, :, :].rearrange("h (pp j) d -> pp h j d", j=TILES)[:, :, first : first + count, :],
-                    in_=o_t[b:P:4, :, :, :],
-                )
-
-        def project_quad(c, q, engines):
             o_t = o_pool.tile([P, 8, 4, 64], F32, name="o_t", tag="o")
-            project(c, q, engines, o_t, 0)
-            store(c, o_t, 4 * q, 4)
+            for jq in range(4):
+                copy_on(engines[jq], o_t[:, :, jq, :], accs[jq][:].rearrange("p a (x d) -> p (a x) d", d=64))
+            for half in range(2):
+                h0 = 8 * (c % 2) + 4 * half
+                for b in range(B):
+                    nc.sync.dma_start(
+                        out=outs[c // 2][b, h0 : h0 + 4, :, :].rearrange("h (pp j) d -> pp h j d", j=TILES)[:, :, 4 * q : 4 * q + 4, :],
+                        in_=o_t[b:P:4, 4 * half : 4 * half + 4, :, :],
+                    )
 
         nc.vector.memset(lnrow[:], 0.0)
         nc.scalar.dma_start(out=lnrow[0:4, :], in_=ln_w.rearrange("(r c) -> r c", c=256))
@@ -231,21 +225,17 @@ def tile_selfattention_pa_kernel(tc, inputs, ln_w, ln_b, w_qkv, out_0, out_1, ou
         prepare_x(0, lambda: w_quantise(0))
         prepare_w(1, "ssss")
         prepare_w(2, "ssss")
-        project_quad(0, 0, "sssv")
+        project(0, 0, "sssv")
         prepare_x(1, None)
-        project_quad(1, 0, "sssv")
-        project_quad(2, 0, "sssv")
-        project_quad(0, 1, "svsv")
-        project_quad(1, 1, "svsv")
+        project(1, 0, "sssv")
+        project(2, 0, "sssv")
+        project(0, 1, "svsv")
+        project(1, 1, "svsv")
         prepare_w(3, "svsv")
-        project_quad(2, 1, "svsv")
+        project(2, 1, "svsv")
         prepare_w(4, "svsv")
-        for c in (3, 4):
-            o_t = o8_pool.tile([P, 8, TILES, 64], F32, name="o8_t", tag="o8")
-            project(c, 0, "svsv", o_t, 0)
+        for c in range(3, CHUNKS):
+            project(c, 0, "svsv")
             if c == 3:
                 prepare_w(5, "svsv")
-            project(c, 1, "svsv", o_t, 4)
-            store(c, o_t, 0, TILES)
-        project_quad(5, 0, "svsv")
-        project_quad(5, 1, "svsv")
+            project(c, 1, "svsv")

from contextlib import ExitStack

import concourse.mybir as mybir
from concourse.masks import make_identity

FLOPS = 2 * 1024 * 3072 * 1024

F32 = mybir.dt.float32
BF16 = mybir.dt.bfloat16
U32 = mybir.dt.uint32
U8 = mybir.dt.uint8
FP8X4 = mybir.dt.float8_e4m3fn_x4
ALU = mybir.AluOpType
ACT = mybir.ActivationFunctionType

P = 128
B = 4
E = 1024
EPS = 1e-5
TILES = 8
CHUNKS = 6


def tile_selfattention_pa_kernel(tc, inputs, ln_w, ln_b, w_qkv, out_0, out_1, out_2):
    nc = tc.nc
    outs = (out_0, out_1, out_2)
    with ExitStack() as ctx:
        const = ctx.enter_context(tc.tile_pool(name="const", bufs=1))
        wraw_pool = ctx.enter_context(tc.tile_pool(name="wraw", bufs=CHUNKS))
        gw_pool = ctx.enter_context(tc.tile_pool(name="gw", bufs=2))
        xh_pool = ctx.enter_context(tc.tile_pool(name="xh", bufs=8))
        pl_pool = ctx.enter_context(tc.tile_pool(name="pl", bufs=2))
        gx_pool = ctx.enter_context(tc.tile_pool(name="gx", bufs=2))
        o_pool = ctx.enter_context(tc.tile_pool(name="o", bufs=6))
        ps_pool = ctx.enter_context(tc.psum_pool(name="ps", bufs=8))
        ctx.enter_context(tc.manual_schedule())

        ident = const.tile([P, P], F32)
        one = const.tile([P, 1], F32)
        warm = const.tile([P, 1], F32)
        lnrow = const.tile([P, 256], BF16)
        lnf = const.tile([P, 2, P], F32)
        wb = const.tile([P, 2, 8], F32)
        x_sb = {}
        xc = const.tile([P, 2 * 2 * 512], U32, align_bytes=64)
        xs = const.tile([P, 2 * 2 * 512], U8, align_bytes=64)
        wc = const.tile([P, CHUNKS * 1024], U32, align_bytes=64)
        ws = const.tile([P, CHUNKS * 1024], U8, align_bytes=64)
        st = const.tile([P, TILES, 2, 6], F32)
        mv = const.tile([P, TILES, 2], F32)
        std = const.tile([P, TILES], F32)
        rstd = const.tile([P, TILES], F32)
        negmu = const.tile([P, TILES], F32)
        wraw = []
        xh = {}

        def copy_on(eng, dst, src):
            if eng == "v":
                nc.vector.tensor_copy(out=dst, in_=src)
            else:
                nc.scalar.copy(out=dst, in_=src)

        def bank():
            return ps_pool.tile([P, 4, P], F32, name="bank", tag="ps")

        def load_x(j0, j1):
            x_t = const.tile([P, j1 - j0, E], BF16, name="x_t%d" % j0)
            for b in range(B):
                nc.sync.dma_start(
                    out=x_t[b:P:4, :, :],
                    in_=inputs[b].rearrange("(pp j) k -> pp j k", j=TILES)[:, j0:j1, :],
                )
            for j in range(j0, j1):
                x_sb[j] = x_t[:, j - j0, :]

        def load_w(c):
            w_t = wraw_pool.tile([P, 4 * E], BF16, name="wraw_t", tag="wraw")
            nc.sync.dma_start(
                out=w_t[:].rearrange("p (r k) -> p r k", r=4),
                in_=w_qkv[512 * c : 512 * c + 512, :].rearrange("(r p) k -> p r k", p=P),
            )
            wraw.append(w_t)

        def statistics(j):
            for h in range(2):
                nc.vector.bn_stats(out=st[:, j, h, :], in_=x_sb[j][:, 512 * h : 512 * h + 512])
            nc.vector.bn_aggr(out=mv[:, j, :], in_=st[:, j, :, :].rearrange("p a b -> p (a b)"))
            nc.scalar.activation(out=std[:, j : j + 1], in_=mv[:, j, 1:2], func=ACT.Sqrt, bias=EPS)

        def normalise(j):
            nc.vector.reciprocal(out=rstd[:, j : j + 1], in_=std[:, j : j + 1])
            nc.vector.tensor_scalar_mul(out=negmu[:, j : j + 1], in0=mv[:, j, 0:1], scalar1=-1.0)
            t = xh_pool.tile([P, 8, P], F32, name="xh_t", tag="xh")
            nc.gpsimd.tensor_scalar(
                out=t[:].rearrange("p (gu e) q -> p gu e q", e=2),
                in0=x_sb[j].rearrange("p (gu q e) -> p gu e q", gu=4, e=2),
                scalar1=negmu[:, j : j + 1],
                scalar2=rstd[:, j : j + 1],
                op0=ALU.add,
                op1=ALU.mult,
            )
            xh[j] = t

        gw = {}

        def w_transposes(c, r):
            t = bank()
            wf = wraw[c][:].bitcast(F32)
            for gu in range(4):
                nc.tensor.transpose(t[:, gu, :], wf[:, 512 * r + P * gu : 512 * r + P * gu + P], ident[:])
            return t

        def w_copy(c, r, t, eng):
            if c not in gw:
                gw[c] = gw_pool.tile([P, 4096], BF16, name="gw_t", tag="gw", align_bytes=64)
            gwf = gw[c][:].bitcast(F32).rearrange("p (g n u) -> p g n u", g=2, u=2)
            copy_on(eng, gwf[:, :, P * r : P * r + P, :], t[:].rearrange("p (g u) f -> p g f u", u=2))

        def w_quantise(c):
            sl = slice(c * 1024, c * 1024 + 1024)
            nc.vector.quantize_mx(out=wc[:, sl].bitcast(FP8X4), scales=ws[:, sl], in_=gw[c][:])

        def prepare_w(c, engines):
            banks = [w_transposes(c, r) for r in range(4)]
            for r in range(4):
                w_copy(c, r, banks[r], engines[r])
            w_quantise(c)

        def x_regroup(planes):
            gx = gx_pool.tile([P, 512, 4], BF16, name="gx_t", tag="gx", align_bytes=64)
            nc.vector.tensor_copy(
                out=gx[:].rearrange("p (c i) t -> p c t i", i=4),
                in_=planes[:].rearrange("p t (c i) -> p c t i", i=4),
            )
            return gx

        def x_quantise(q, g, gx):
            sl = slice((2 * q + g) * 512, (2 * q + g) * 512 + 512)
            nc.vector.quantize_mx(out=xc[:, sl].bitcast(FP8X4), scales=xs[:, sl], in_=gx[:].rearrange("p n t -> p (n t)"))

        def prepare_x(q, between):
            planes = [pl_pool.tile([P, 4, 512], BF16, name="planes", tag="pl") for g in range(2)]
            gx = [None, None]
            for t in range(8):
                g, t4 = t // 4, t % 4
                gu, e = t // 2, t % 2
                xt = bank()
                for jq in range(4):
                    nc.tensor.transpose(xt[:, jq, :], xh[4 * q + jq][:, t, :], ident[:])
                src = xt[:].rearrange("p a b -> p (a b)")
                if t % 2 == 1:
                    nc.vector.tensor_scalar(
                        out=planes[g][:, t4, :], in0=src,
                        scalar1=wb[:, e, gu : gu + 1], scalar2=wb[:, e, 4 + gu : 5 + gu],
                        op0=ALU.mult, op1=ALU.add,
                    )
                else:
                    nc.scalar.activation(
                        out=planes[g][:, t4, :], in_=src, func=ACT.Identity,
                        scale=wb[:, e, gu : gu + 1], bias=wb[:, e, 4 + gu : 5 + gu],
                    )
                if t == 3 and between is not None:
                    between()
                if t == 5:
                    gx[0] = x_regroup(planes[0])
            gx[1] = x_regroup(planes[1])
            x_quantise(q, 0, gx[0])
            x_quantise(q, 1, gx[1])

        def project(c, q, engines):
            accs = []
            for jq in range(4):
                acc = bank()
                for g in range(2):
                    xo = (2 * q + g) * 512 + P * jq
                    wo = c * 1024 + 512 * g
                    nc.tensor.matmul_mx(
                        out=acc[:].rearrange("p a b -> p (a b)"),
                        lhsT=xc[:, xo : xo + P].bitcast(FP8X4), lhsT_scale=xs[:, xo : xo + P],
                        rhs=wc[:, wo : wo + 512].bitcast(FP8X4), rhs_scale=ws[:, wo : wo + 512],
                        start=(g == 0), stop=(g == 1),
                    )
                accs.append(acc)
            o_t = o_pool.tile([P, 8, 4, 64], F32, name="o_t", tag="o")
            for jq in range(4):
                copy_on(engines[jq], o_t[:, :, jq, :], accs[jq][:].rearrange("p a (x d) -> p (a x) d", d=64))
            for half in range(2):
                h0 = 8 * (c % 2) + 4 * half
                for b in range(B):
                    nc.sync.dma_start(
                        out=outs[c // 2][b, h0 : h0 + 4, :, :].rearrange("h (pp j) d -> pp h j d", j=TILES)[:, :, 4 * q : 4 * q + 4, :],
                        in_=o_t[b:P:4, 4 * half : 4 * half + 4, :, :],
                    )

        nc.vector.memset(lnrow[:], 0.0)
        nc.scalar.dma_start(out=lnrow[0:4, :], in_=ln_w.rearrange("(r c) -> r c", c=256))
        nc.scalar.dma_start(out=lnrow[4:8, :], in_=ln_b.rearrange("(r c) -> r c", c=256))
        load_x(0, 1)
        load_x(1, 2)
        load_x(2, 4)
        load_w(0)
        load_x(4, 8)
        for c in range(1, CHUNKS):
            load_w(c)
        make_identity(nc, ident[:])
        nc.vector.memset(one[:], 1.0)
        nc.scalar.activation(out=warm[:], in_=one[:], func=ACT.Sqrt)

        for k in range(TILES + 1):
            if k < TILES:
                statistics(k)
            if k >= 1:
                normalise(k - 1)
            if k == 1:
                nc.vector.tensor_copy(out=lnf[:], in_=lnrow[:].rearrange("p (q e) -> p e q", e=2))
                lnt = bank()
                for e in range(2):
                    nc.tensor.transpose(lnt[:, e, :], lnf[:, e, :], ident[:])
            if k == 2:
                nc.vector.tensor_copy(out=wb[:], in_=lnt[:, 0:2, 0:8])
            if k in (3, 4):
                for r in (2 * (k - 3), 2 * (k - 3) + 1):
                    w_copy(0, r, w_transposes(0, r), "s")

        prepare_x(0, lambda: w_quantise(0))
        prepare_w(1, "ssss")
        prepare_w(2, "ssss")
        project(0, 0, "sssv")
        prepare_x(1, None)
        project(1, 0, "sssv")
        project(2, 0, "sssv")
        project(0, 1, "svsv")
        project(1, 1, "svsv")
        prepare_w(3, "svsv")
        project(2, 1, "svsv")
        prepare_w(4, "svsv")
        for c in range(3, CHUNKS):
            project(c, 0, "svsv")
            if c == 3:
                prepare_w(5, "svsv")
            project(c, 1, "svsv")
